import numpy as np
import ml_dtypes


def mxq(x, axis, fmt="e4m3"):
    dtype, down = {"e4m3": (ml_dtypes.float8_e4m3fn, 7), "e5m2": (ml_dtypes.float8_e5m2, 14)}[fmt]
    v = np.moveaxis(np.asarray(x, np.float32).astype(ml_dtypes.bfloat16).astype(np.float64), axis, -1)
    blocks = v.reshape(v.shape[:-1] + (-1, 32))
    amax = np.abs(blocks).max(-1, keepdims=True)
    byte = np.maximum(np.where(amax > 0, np.frexp(amax)[1] - 1 + 127, 0) - down, 1)
    scale = np.exp2(byte - 127.0)
    codes = (blocks / scale).astype(np.float32).astype(dtype).astype(np.float64)
    return np.moveaxis((codes * scale).reshape(v.shape), -1, axis)


WIDE = False


def mx_kscale(k):
    if not WIDE:
        return np.ones(k)
    levels = np.array([10, -10, 5, -5, 0])
    a = np.random.permutation(np.resize(levels, k // 512 * 4)).reshape(k // 512, 4)
    idx = np.arange(k)
    return np.exp2(a[idx // 512, idx % 128 // 32])


BF16 = ml_dtypes.bfloat16


def bf(x):
    return np.asarray(x, np.float32).astype(BF16)


def f64(x):
    return np.asarray(x).astype(np.float64)


B, A, S, F = 512, 16, 256, 512


def setup_inputs():
    s, u = mx_kscale(F), mx_kscale(F)
    t, v = mx_kscale(F), mx_kscale(F)
    return {
        "h1": bf(np.maximum(np.random.standard_normal((B, A, F)) * 1.4, 0.0) * s),
        "W2": bf(np.random.standard_normal((A, F, F)) * 1.4 / np.sqrt(F) / s[:, None] * t),
        "b2": bf(np.random.standard_normal((A, F)) * 0.2 * t),
        "W3": bf(np.random.standard_normal((A, F, S)) / np.sqrt(F) / t[:, None]),
        "b3": bf(np.random.standard_normal((A, S)) * 0.2),
        "g1": bf(np.maximum(np.random.standard_normal((B, F)) * 1.4, 0.0) * u),
        "V2": bf(np.random.standard_normal((F, F)) * 1.4 / np.sqrt(F) / u[:, None] * v),
        "c2": bf(np.random.standard_normal(F) * 0.2 * v),
        "V3": bf(np.random.standard_normal((F, S)) / np.sqrt(F) / v[:, None]),
        "c3": bf(np.random.standard_normal(S) * 0.2),
    }


def reference(h1, W2, b2, W3, b3, g1, V2, c2, V3, c3):
    ha = mxq(f64(h1), 2, "e4m3").transpose(1, 0, 2)
    h2 = np.maximum((ha @ mxq(f64(W2), 1, "e4m3")) + f64(b2)[:, None, :], 0.0)
    psi_adv = ((mxq(h2, 2, "e4m3") @ mxq(f64(W3), 1, "e4m3")) + f64(b3)[:, None, :]).transpose(1, 0, 2)
    g2 = np.maximum((mxq(f64(g1), 1, "e4m3") @ mxq(f64(V2), 0, "e4m3")) + f64(c2), 0.0)
    psi_state = (mxq(g2, 1, "e4m3") @ mxq(f64(V3), 0, "e4m3")) + f64(c3)
    return psi_state[:, None, :] + psi_adv - psi_adv.mean(axis=1, keepdims=True)

@@ -1,0 +1,295 @@
+from contextlib import ExitStack
+
+import concourse.mybir as mybir
+from concourse.masks import make_identity
+
+FLOPS = 17 * (2 * 512 * 512 * 512 + 2 * 512 * 512 * 256)
+
+F32 = mybir.dt.float32
+BF16 = mybir.dt.bfloat16
+U32 = mybir.dt.uint32
+U8 = mybir.dt.uint8
+FP8X4 = mybir.dt.float8_e4m3fn_x4
+ADD = mybir.AluOpType.add
+MULT = mybir.AluOpType.mult
+RELU = mybir.ActivationFunctionType.Relu
+
+P = 128
+A = 16
+NI = 4
+F = 512
+S = 256
+HV = 384
+NW = A + 1
+
+
+def regroup(engine_copy, dst, src):
+    engine_copy(
+        out=dst.rearrange("p (c i) t -> p c t i", i=4),
+        in_=src.rearrange("p t (c i) -> p c t i", i=4),
+    )
+
+
+def tile_psicritic_pa_kernel(tc, h1, W2, b2, W3, b3, g1, V2, c2, V3, c3, out):
+    nc = tc.nc
+    h1v = h1.rearrange("(i p) a k -> p i a k", p=P)
+    outv = out.rearrange("(i p) a s -> p i a s", p=P)
+
+    with ExitStack() as ctx:
+        const = ctx.enter_context(tc.tile_pool(name="const", bufs=1))
+        xpool = ctx.enter_context(tc.tile_pool(name="xpool", bufs=3))
+        rawp = ctx.enter_context(tc.tile_pool(name="rawp", bufs=4))
+        grp = ctx.enter_context(tc.tile_pool(name="grp", bufs=2))
+        wcode = ctx.enter_context(tc.tile_pool(name="wcode", bufs=4))
+        acode = ctx.enter_context(tc.tile_pool(name="acode", bufs=2))
+        tp_pool = ctx.enter_context(tc.psum_pool(name="tp_pool", bufs=2))
+        l1_pool = ctx.enter_context(tc.psum_pool(name="l1_pool", bufs=3))
+        pp_pool = ctx.enter_context(tc.psum_pool(name="pp_pool", bufs=1))
+        m_pool = ctx.enter_context(tc.psum_pool(name="m_pool", bufs=1))
+
+        brow = const.tile([P, P], BF16, name="brow")
+        nc.vector.memset(brow[:], 0.0)
+        nc.gpsimd.dma_start(out=brow[0:4, :], in_=c2.rearrange("(t p) -> t p", p=P))
+        nc.gpsimd.dma_start(out=brow[4:68, :], in_=b2.rearrange("a (t p) -> (a t) p", p=P))
+        b3rows = const.tile([P, S], BF16, name="b3rows")
+        nc.vector.memset(b3rows[:], 0.0)
+        nc.gpsimd.dma_start(out=b3rows[0:16, :], in_=b3)
+        nc.gpsimd.dma_start(out=b3rows[16:17, :], in_=c3.rearrange("(o s) -> o s", o=1))
+        b3bc = const.tile([P, A, S], BF16, name="b3bc")
+        nc.gpsimd.dma_start(
+            out=b3bc[:].rearrange("p a s -> p (a s)"),
+            in_=b3.rearrange("a s -> (a s)").partition_broadcast(P),
+        )
+        ident = const.tile([P, P], F32, name="ident")
+        make_identity(nc, ident[:])
+        lmean = const.tile([P, P], BF16, name="lmean")
+        nc.vector.memset(lmean[:], 0.0)
+        nc.vector.memset(lmean[0:17, :], 1.0)
+        nc.vector.memset(lmean[0:16, :], -1.0 / A)
+
+        xg = const.tile([P, NI, F], BF16, name="xg")
+
+        raws = {}
+
+        def load_w(w):
+            w2src = V2 if w == 0 else W2[w - 1]
+            w3src = V3 if w == 0 else W3[w - 1]
+            w2raw = rawp.tile([P, 4, F], BF16, name="w2raw")
+            nc.sync.dma_start(
+                out=w2raw[:].rearrange("p (u e) n -> p u (e n)", u=2),
+                in_=w2src.rearrange("(u p e) n -> p u (e n)", u=2, e=2),
+            )
+            w3raw = rawp.tile([P, 4, S], BF16, name="w3raw")
+            nc.sync.dma_start(out=w3raw[:], in_=w3src.rearrange("(t p) s -> p t s", p=P))
+            raws[w] = (w2raw, w3raw)
+
+        xs = {}
+
+        def load_x(pair):
+            xt = xpool.tile([P, NI, 2, F], BF16, name="xt")
+            nc.sync.dma_start(out=xt[:], in_=h1v[:, :, 2 * pair : 2 * pair + 2, :])
+            xs[pair] = xt
+
+        nc.sync.dma_start(out=xg[:], in_=g1.rearrange("(i p) k -> p i k", p=P))
+        load_w(0)
+        load_x(0)
+        load_w(1)
+        load_w(2)
+
+        browf = const.tile([P, P], F32, name="browf")
+        nc.vector.tensor_copy(out=browf[:], in_=brow[:])
+        tpb = tp_pool.tile([P, 2, S], F32, name="tpb", tag="tp")
+        nc.tensor.transpose(tpb[:, 0, 0:P], browf[:], ident[:])
+        bias2 = const.tile([P, P], F32, name="bias2")
+        nc.vector.tensor_copy(out=bias2[:], in_=tpb[:, 0, 0:P])
+
+        tpg = tp_pool.tile([P, 2, S], F32, name="tpg", tag="tp")
+        nc.tensor.matmul(tpg[:, 0, :], lhsT=lmean[:], rhs=b3rows[:], start=True, stop=True)
+        gam = const.tile([P, S], F32, name="gam")
+        nc.vector.tensor_copy(out=gam[:], in_=tpg[:, 0, :])
+
+        outsb = const.tile([P, NI, A, S], F32, name="outsb")
+        sg = const.tile([P, NI, S], F32, name="sg")
+        dpre = const.tile([P, NI, S], F32, name="dpre")
+        dfin = const.tile([P, NI, S], F32, name="dfin")
+        mts = const.tile([P, 2, F], F32, name="mts")
+        mt = [m_pool.tile([P, F], F32, name="mt%d" % st) for st in range(2)]
+
+        wc = {}
+
+        def prep_w(w):
+            w2raw, w3raw = raws[w]
+            w2g = grp.tile([P, F, 4], BF16, name="w2g", align_bytes=64)
+            regroup(nc.vector.tensor_copy, w2g[:], w2raw[:])
+            w3g = grp.tile([P, S, 4], BF16, name="w3g", align_bytes=64)
+            regroup(nc.scalar.copy, w3g[:], w3raw[:])
+            w2c = wcode.tile([P, F], U32, name="w2c", align_bytes=64)
+            w2s = wcode.tile([P, F], U8, name="w2s", align_bytes=64)
+            nc.vector.quantize_mx(
+                out=w2c[:].bitcast(FP8X4), scales=w2s[:], in_=w2g[:].rearrange("p n t -> p (n t)")
+            )
+            w3c = wcode.tile([P, S], U32, name="w3c", align_bytes=64)
+            w3s = wcode.tile([P, S], U8, name="w3s", align_bytes=64)
+            nc.vector.quantize_mx(
+                out=w3c[:].bitcast(FP8X4), scales=w3s[:], in_=w3g[:].rearrange("p n t -> p (n t)")
+            )
+            wc[w] = (w2c, w2s, w3c, w3s)
+
+        hc = {}
+
+        def front(w):
+            if w == 0:
+                xw = xg[:].bitcast(F32)
+            else:
+                a = w - 1
+                xw = xs[a // 2][:].bitcast(F32)[:, :, a % 2, :]
+            g1t = grp.tile([P, F, 4], BF16, name="g1t", align_bytes=64)
+            g1w = g1t[:].bitcast(F32)
+            for ih in range(2):
+                tp = tp_pool.tile([P, 2, S], F32, name="tp", tag="tp")
+                for il in range(2):
+                    for u in range(2):
+                        nc.tensor.transpose(
+                            tp[:, u, P * il : P * il + P],
+                            xw[:, 2 * ih + il, P * u : P * u + P],
+                            ident[:],
+                        )
+                nc.scalar.copy(
+                    out=g1w[:, S * ih : S * ih + S, :], in_=tp[:].rearrange("p u b -> p b u")
+                )
+            h1c = acode.tile([P, F], U32, name="h1c", align_bytes=64)
+            h1s = acode.tile([P, F], U8, name="h1s", align_bytes=64)
+            nc.vector.quantize_mx(
+                out=h1c[:].bitcast(FP8X4), scales=h1s[:], in_=g1t[:].rearrange("p n t -> p (n t)")
+            )
+            hc[w] = (h1c, h1s)
+
+        h2 = {}
+
+        def mid(w):
+            w2c, w2s, w3c, w3s = wc[w]
+            h1c, h1s = hc[w]
+            planes = grp.tile([P, 4, F], BF16, name="planes")
+            for t in range(4):
+                l1 = l1_pool.tile([P, F], F32, name="l1")
+                nc.tensor.matmul_mx(
+                    out=l1[:],
+                    lhsT=w2c[:, P * t : P * t + P].bitcast(FP8X4),
+                    lhsT_scale=w2s[:, P * t : P * t + P],
+                    rhs=h1c[:].bitcast(FP8X4),
+                    rhs_scale=h1s[:],
+                    start=True,
+                    stop=True,
+                )
+                nc.scalar.activation(
+                    out=planes[:, t, :],
+                    in_=l1[:],
+                    func=RELU,
+                    bias=bias2[:, 4 * w + t : 4 * w + t + 1],
+                    scale=1.0,
+                )
+            g2t = grp.tile([P, F, 4], BF16, name="g2t", align_bytes=64)
+            regroup(nc.vector.tensor_copy, g2t[:, 0:HV, :], planes[:, :, 0:HV])
+            regroup(nc.scalar.copy, g2t[:, HV:F, :], planes[:, :, HV:F])
+            h2c = acode.tile([P, F], U32, name="h2c", align_bytes=64)
+            h2s = acode.tile([P, F], U8, name="h2s", align_bytes=64)
+            nc.vector.quantize_mx(
+                out=h2c[:].bitcast(FP8X4), scales=h2s[:], in_=g2t[:].rearrange("p n t -> p (n t)")
+            )
+            h2[w] = (h2c, h2s)
+
+        def back(w):
+            w2c, w2s, w3c, w3s = wc[w]
+            h2c, h2s = h2[w]
+            a = w - 1
+            for ih in range(2):
+                pp = pp_pool.tile([P, 2, S], F32, name="pp")
+                for il in range(2):
+                    i = 2 * ih + il
+                    nc.tensor.matmul_mx(
+                        out=pp[:, il, :],
+                        lhsT=h2c[:, P * i : P * i + P].bitcast(FP8X4),
+                        lhsT_scale=h2s[:, P * i : P * i + P],
+                        rhs=w3c[:].bitcast(FP8X4),
+                        rhs_scale=w3s[:],
+                        start=True,
+                        stop=True,
+                    )
+                pair = slice(2 * ih, 2 * ih + 2)
+                if w == 0:
+                    nc.vector.tensor_tensor(
+                        out=sg[:, pair, :],
+                        in0=pp[:],
+                        in1=gam[:].unsqueeze(1).to_broadcast([P, 2, S]),
+                        op=ADD,
+                    )
+                else:
+                    if a == A - 1:
+                        nc.vector.scalar_tensor_tensor(
+                            out=dfin[:, pair, :],
+                            in0=pp[:],
+                            scalar=-1.0 / A,
+                            in1=dpre[:, pair, :],
+                            op0=MULT,
+                            op1=ADD,
+                        )
+                    nc.vector.tensor_tensor(
+                        out=outsb[:, pair, a, :],
+                        in0=pp[:],
+                        in1=b3bc[:, a, :].unsqueeze(1).to_broadcast([P, 2, S]),
+                        op=ADD,
+                    )
+            if 1 <= w <= A - 1:
+                for st in range(2):
+                    nc.tensor.matmul_mx(
+                        out=mt[st][:],
+                        lhsT=w3c[:, P * st : P * st + P].bitcast(FP8X4),
+                        lhsT_scale=w3s[:, P * st : P * st + P],
+                        rhs=h2c[:].bitcast(FP8X4),
+                        rhs_scale=h2s[:],
+                        start=(w == 1),
+                        stop=(w == A - 1),
+                    )
+            if w == A - 1:
+                for st in range(2):
+                    nc.scalar.copy(out=mts[:, st, :], in_=mt[st][:])
+                for ih in range(2):
+                    mb = tp_pool.tile([P, 2, S], F32, name="mb", tag="tp")
+                    for il in range(2):
+                        i = 2 * ih + il
+                        for st in range(2):
+                            nc.tensor.transpose(
+                                mb[:, il, P * st : P * st + P],
+                                mts[:, st, P * i : P * i + P],
+                                ident[:],
+                            )
+                    pair = slice(2 * ih, 2 * ih + 2)
+                    nc.vector.scalar_tensor_tensor(
+                        out=dpre[:, pair, :],
+                        in0=mb[:],
+                        scalar=-1.0 / A,
+                        in1=sg[:, pair, :],
+                        op0=MULT,
+                        op1=ADD,
+                    )
+
+        for w in range(NW):
+            if w + 3 < NW:
+                load_w(w + 3)
+            if w % 2 == 0 and w // 2 + 1 < A // 2:
+                load_x(w // 2 + 1)
+            prep_w(w)
+            front(w)
+            mid(w)
+            back(w)
+
+        for i in range(NI):
+            for c in range(4):
+                acts = slice(4 * c, 4 * c + 4)
+                nc.vector.tensor_tensor(
+                    out=outsb[:, i, acts, :],
+                    in0=outsb[:, i, acts, :],
+                    in1=dfin[:, i, :].unsqueeze(1).to_broadcast([P, 4, S]),
+                    op=ADD,
+                )
+                nc.sync.dma_start(out=outv[:, i, acts, :], in_=outsb[:, i, acts, :])

@@ -21,6 +21,8 @@ F = 512
 S = 256
 HV = 384
 NW = A + 1
+RAW_BUFS = 4
+X_BUFS = 3
 
 
 def regroup(engine_copy, dst, src):
@@ -37,73 +39,92 @@ def tile_psicritic_pa_kernel(tc, h1, W2, b2, W3, b3, g1, V2, c2, V3, c3, out):
 
     with ExitStack() as ctx:
         const = ctx.enter_context(tc.tile_pool(name="const", bufs=1))
-        xpool = ctx.enter_context(tc.tile_pool(name="xpool", bufs=3))
-        rawp = ctx.enter_context(tc.tile_pool(name="rawp", bufs=4))
-        grp = ctx.enter_context(tc.tile_pool(name="grp", bufs=2))
-        wcode = ctx.enter_context(tc.tile_pool(name="wcode", bufs=4))
-        acode = ctx.enter_context(tc.tile_pool(name="acode", bufs=2))
+        xpool = ctx.enter_context(tc.tile_pool(name="xpool", bufs=X_BUFS))
+        rawp = ctx.enter_context(tc.tile_pool(name="rawp", bufs=RAW_BUFS))
+        two = ctx.enter_context(tc.tile_pool(name="two", bufs=2))
+        three = ctx.enter_context(tc.tile_pool(name="three", bufs=3))
         tp_pool = ctx.enter_context(tc.psum_pool(name="tp_pool", bufs=2))
-        l1_pool = ctx.enter_context(tc.psum_pool(name="l1_pool", bufs=3))
-        pp_pool = ctx.enter_context(tc.psum_pool(name="pp_pool", bufs=1))
+        l1_pool = ctx.enter_context(tc.psum_pool(name="l1_pool", bufs=2))
+        pp_pool = ctx.enter_context(tc.psum_pool(name="pp_pool", bufs=2))
         m_pool = ctx.enter_context(tc.psum_pool(name="m_pool", bufs=1))
-
-        brow = const.tile([P, P], BF16, name="brow")
-        nc.vector.memset(brow[:], 0.0)
-        nc.gpsimd.dma_start(out=brow[0:4, :], in_=c2.rearrange("(t p) -> t p", p=P))
-        nc.gpsimd.dma_start(out=brow[4:68, :], in_=b2.rearrange("a (t p) -> (a t) p", p=P))
-        b3rows = const.tile([P, S], BF16, name="b3rows")
-        nc.vector.memset(b3rows[:], 0.0)
-        nc.gpsimd.dma_start(out=b3rows[0:16, :], in_=b3)
-        nc.gpsimd.dma_start(out=b3rows[16:17, :], in_=c3.rearrange("(o s) -> o s", o=1))
-        b3bc = const.tile([P, A, S], BF16, name="b3bc")
-        nc.gpsimd.dma_start(
-            out=b3bc[:].rearrange("p a s -> p (a s)"),
-            in_=b3.rearrange("a s -> (a s)").partition_broadcast(P),
-        )
-        ident = const.tile([P, P], F32, name="ident")
-        make_identity(nc, ident[:])
-        lmean = const.tile([P, P], BF16, name="lmean")
-        nc.vector.memset(lmean[:], 0.0)
-        nc.vector.memset(lmean[0:17, :], 1.0)
-        nc.vector.memset(lmean[0:16, :], -1.0 / A)
-
-        xg = const.tile([P, NI, F], BF16, name="xg")
+        ctx.enter_context(tc.manual_schedule())
 
         raws = {}
+        xs = {}
+        wg = {}
+        w2q = {}
+        w3q = {}
+        g1s = {}
+        h1q = {}
+        pls = {}
+        g2s = {}
+        h2q = {}
+        pps = {}
 
-        def load_w(w):
-            w2src = V2 if w == 0 else W2[w - 1]
-            w3src = V3 if w == 0 else W3[w - 1]
+        def live(w):
+            return 0 <= w < NW
+
+        def load_w2(w):
             w2raw = rawp.tile([P, 4, F], BF16, name="w2raw")
             nc.sync.dma_start(
                 out=w2raw[:].rearrange("p (u e) n -> p u (e n)", u=2),
-                in_=w2src.rearrange("(u p e) n -> p u (e n)", u=2, e=2),
+                in_=(V2 if w == 0 else W2[w - 1]).rearrange("(u p e) n -> p u (e n)", u=2, e=2),
             )
-            w3raw = rawp.tile([P, 4, S], BF16, name="w3raw")
-            nc.sync.dma_start(out=w3raw[:], in_=w3src.rearrange("(t p) s -> p t s", p=P))
-            raws[w] = (w2raw, w3raw)
+            raws[(2, w)] = w2raw
 
-        xs = {}
+        def load_w3(w):
+            w3raw = rawp.tile([P, 4, S], BF16, name="w3raw")
+            nc.sync.dma_start(
+                out=w3raw[:], in_=(V3 if w == 0 else W3[w - 1]).rearrange("(t p) s -> p t s", p=P)
+            )
+            raws[(3, w)] = w3raw
 
         def load_x(pair):
             xt = xpool.tile([P, NI, 2, F], BF16, name="xt")
             nc.sync.dma_start(out=xt[:], in_=h1v[:, :, 2 * pair : 2 * pair + 2, :])
             xs[pair] = xt
 
+        ident = const.tile([P, P], F32, name="ident")
+        make_identity(nc, ident[:])
+        brow = const.tile([P, P], BF16, name="brow")
+        nc.vector.memset(brow[:], 0.0)
+        nc.scalar.dma_start(out=brow[0:4, :], in_=c2.rearrange("(t p) -> t p", p=P))
+        nc.scalar.dma_start(out=brow[4:68, :], in_=b2.rearrange("a (t p) -> (a t) p", p=P))
+        b3rows = const.tile([P, S], BF16, name="b3rows")
+        nc.vector.memset(b3rows[:], 0.0)
+        nc.scalar.dma_start(out=b3rows[0:16, :], in_=b3)
+        nc.scalar.dma_start(out=b3rows[16:17, :], in_=c3.rearrange("(o s) -> o s", o=1))
+        lmean = const.tile([P, P], BF16, name="lmean")
+        nc.vector.memset(lmean[:], 0.0)
+        nc.vector.memset(lmean[0:17, :], 1.0)
+        nc.vector.memset(lmean[0:16, :], -1.0 / A)
+
+        xg = const.tile([P, NI, F], BF16, name="xg")
+        b3bc = const.tile([P, A, S], BF16, name="b3bc")
+        load_w2(0)
         nc.sync.dma_start(out=xg[:], in_=g1.rearrange("(i p) k -> p i k", p=P))
-        load_w(0)
+        load_w3(0)
+        load_w2(1)
         load_x(0)
-        load_w(1)
-        load_w(2)
+        load_w3(1)
+        load_w2(2)
+        load_w3(2)
+        nc.sync.dma_start(
+            out=b3bc[:].rearrange("p a s -> p (a s)"),
+            in_=b3.rearrange("a s -> (a s)").partition_broadcast(P),
+        )
+        load_x(1)
+        load_w2(3)
+        load_w3(3)
+        load_x(2)
 
         browf = const.tile([P, P], F32, name="browf")
         nc.vector.tensor_copy(out=browf[:], in_=brow[:])
-        tpb = tp_pool.tile([P, 2, S], F32, name="tpb", tag="tp")
+        tpb = pp_pool.tile([P, 2, S], F32, name="tpb", tag="pp")
         nc.tensor.transpose(tpb[:, 0, 0:P], browf[:], ident[:])
         bias2 = const.tile([P, P], F32, name="bias2")
         nc.vector.tensor_copy(out=bias2[:], in_=tpb[:, 0, 0:P])
-
-        tpg = tp_pool.tile([P, 2, S], F32, name="tpg", tag="tp")
+        tpg = pp_pool.tile([P, 2, S], F32, name="tpg", tag="pp")
         nc.tensor.matmul(tpg[:, 0, :], lhsT=lmean[:], rhs=b3rows[:], start=True, stop=True)
         gam = const.tile([P, S], F32, name="gam")
         nc.vector.tensor_copy(out=gam[:], in_=tpg[:, 0, :])
@@ -115,35 +136,27 @@ def tile_psicritic_pa_kernel(tc, h1, W2, b2, W3, b3, g1, V2, c2, V3, c3, out):
         mts = const.tile([P, 2, F], F32, name="mts")
         mt = [m_pool.tile([P, F], F32, name="mt%d" % st) for st in range(2)]
 
-        wc = {}
-
-        def prep_w(w):
-            w2raw, w3raw = raws[w]
-            w2g = grp.tile([P, F, 4], BF16, name="w2g", align_bytes=64)
-            regroup(nc.vector.tensor_copy, w2g[:], w2raw[:])
-            w3g = grp.tile([P, S, 4], BF16, name="w3g", align_bytes=64)
-            regroup(nc.scalar.copy, w3g[:], w3raw[:])
-            w2c = wcode.tile([P, F], U32, name="w2c", align_bytes=64)
-            w2s = wcode.tile([P, F], U8, name="w2s", align_bytes=64)
+        def quantise(pool, width, src, cname, sname):
+            codes = pool.tile([P, width], U32, name=cname, align_bytes=64)
+            scales = pool.tile([P, width], U8, name=sname, align_bytes=64)
             nc.vector.quantize_mx(
-                out=w2c[:].bitcast(FP8X4), scales=w2s[:], in_=w2g[:].rearrange("p n t -> p (n t)")
+                out=codes[:].bitcast(FP8X4), scales=scales[:], in_=src[:].rearrange("p n t -> p (n t)")
             )
-            w3c = wcode.tile([P, S], U32, name="w3c", align_bytes=64)
-            w3s = wcode.tile([P, S], U8, name="w3s", align_bytes=64)
-            nc.vector.quantize_mx(
-                out=w3c[:].bitcast(FP8X4), scales=w3s[:], in_=w3g[:].rearrange("p n t -> p (n t)")
-            )
-            wc[w] = (w2c, w2s, w3c, w3s)
+            return codes, scales
 
-        hc = {}
+        def regroup_weights(w):
+            w2g = two.tile([P, F, 4], BF16, name="w2g", align_bytes=64)
+            regroup(nc.vector.tensor_copy, w2g[:], raws[(2, w)][:])
+            w3g = two.tile([P, S, 4], BF16, name="w3g", align_bytes=64)
+            regroup(nc.scalar.copy, w3g[:], raws[(3, w)][:])
+            wg[w] = (w2g, w3g)
 
-        def front(w):
+        def transpose_x(w):
             if w == 0:
                 xw = xg[:].bitcast(F32)
             else:
-                a = w - 1
-                xw = xs[a // 2][:].bitcast(F32)[:, :, a % 2, :]
-            g1t = grp.tile([P, F, 4], BF16, name="g1t", align_bytes=64)
+                xw = xs[(w - 1) // 2][:].bitcast(F32)[:, :, (w - 1) % 2, :]
+            g1t = two.tile([P, F, 4], BF16, name="g1t", align_bytes=64)
             g1w = g1t[:].bitcast(F32)
             for ih in range(2):
                 tp = tp_pool.tile([P, 2, S], F32, name="tp", tag="tp")
@@ -157,19 +170,12 @@ def tile_psicritic_pa_kernel(tc, h1, W2, b2, W3, b3, g1, V2, c2, V3, c3, out):
                 nc.scalar.copy(
                     out=g1w[:, S * ih : S * ih + S, :], in_=tp[:].rearrange("p u b -> p b u")
                 )
-            h1c = acode.tile([P, F], U32, name="h1c", align_bytes=64)
-            h1s = acode.tile([P, F], U8, name="h1s", align_bytes=64)
-            nc.vector.quantize_mx(
-                out=h1c[:].bitcast(FP8X4), scales=h1s[:], in_=g1t[:].rearrange("p n t -> p (n t)")
-            )
-            hc[w] = (h1c, h1s)
+            g1s[w] = g1t
 
-        h2 = {}
-
-        def mid(w):
-            w2c, w2s, w3c, w3s = wc[w]
-            h1c, h1s = hc[w]
-            planes = grp.tile([P, 4, F], BF16, name="planes")
+        def layer1(w):
+            w2c, w2s = w2q[w]
+            h1c, h1s = h1q[w]
+            planes = two.tile([P, 4, F], BF16, name="planes")
             for t in range(4):
                 l1 = l1_pool.tile([P, F], F32, name="l1")
                 nc.tensor.matmul_mx(
@@ -188,22 +194,19 @@ def tile_psicritic_pa_kernel(tc, h1, W2, b2, W3, b3, g1, V2, c2, V3, c3, out):
                     bias=bias2[:, 4 * w + t : 4 * w + t + 1],
                     scale=1.0,
                 )
-            g2t = grp.tile([P, F, 4], BF16, name="g2t", align_bytes=64)
-            regroup(nc.vector.tensor_copy, g2t[:, 0:HV, :], planes[:, :, 0:HV])
-            regroup(nc.scalar.copy, g2t[:, HV:F, :], planes[:, :, HV:F])
-            h2c = acode.tile([P, F], U32, name="h2c", align_bytes=64)
-            h2s = acode.tile([P, F], U8, name="h2s", align_bytes=64)
-            nc.vector.quantize_mx(
-                out=h2c[:].bitcast(FP8X4), scales=h2s[:], in_=g2t[:].rearrange("p n t -> p (n t)")
-            )
-            h2[w] = (h2c, h2s)
+            pls[w] = planes
 
-        def back(w):
-            w2c, w2s, w3c, w3s = wc[w]
-            h2c, h2s = h2[w]
-            a = w - 1
+        def regroup_hidden(w):
+            g2t = two.tile([P, F, 4], BF16, name="g2t", align_bytes=64)
+            regroup(nc.scalar.copy, g2t[:, HV:F, :], pls[w][:, :, HV:F])
+            regroup(nc.vector.tensor_copy, g2t[:, 0:HV, :], pls[w][:, :, 0:HV])
+            g2s[w] = g2t
+
+        def layer2(w):
+            w3c, w3s = w3q[w]
+            h2c, h2s = h2q[w]
             for ih in range(2):
-                pp = pp_pool.tile([P, 2, S], F32, name="pp")
+                pp = pp_pool.tile([P, 2, S], F32, name="pp", tag="pp")
                 for il in range(2):
                     i = 2 * ih + il
                     nc.tensor.matmul_mx(
@@ -215,30 +218,7 @@ def tile_psicritic_pa_kernel(tc, h1, W2, b2, W3, b3, g1, V2, c2, V3, c3, out):
                         start=True,
                         stop=True,
                     )
-                pair = slice(2 * ih, 2 * ih + 2)
-                if w == 0:
-                    nc.vector.tensor_tensor(
-                        out=sg[:, pair, :],
-                        in0=pp[:],
-                        in1=gam[:].unsqueeze(1).to_broadcast([P, 2, S]),
-                        op=ADD,
-                    )
-                else:
-                    if a == A - 1:
-                        nc.vector.scalar_tensor_tensor(
-                            out=dfin[:, pair, :],
-                            in0=pp[:],
-                            scalar=-1.0 / A,
-                            in1=dpre[:, pair, :],
-                            op0=MULT,
-                            op1=ADD,
-                        )
-                    nc.vector.tensor_tensor(
-                        out=outsb[:, pair, a, :],
-                        in0=pp[:],
-                        in1=b3bc[:, a, :].unsqueeze(1).to_broadcast([P, 2, S]),
-                        op=ADD,
-                    )
+                pps[(w, ih)] = pp
             if 1 <= w <= A - 1:
                 for st in range(2):
                     nc.tensor.matmul_mx(
@@ -250,40 +230,35 @@ def tile_psicritic_pa_kernel(tc, h1, W2, b2, W3, b3, g1, V2, c2, V3, c3, out):
                         start=(w == 1),
                         stop=(w == A - 1),
                     )
-            if w == A - 1:
-                for st in range(2):
-                    nc.scalar.copy(out=mts[:, st, :], in_=mt[st][:])
-                for ih in range(2):
-                    mb = tp_pool.tile([P, 2, S], F32, name="mb", tag="tp")
-                    for il in range(2):
-                        i = 2 * ih + il
-                        for st in range(2):
-                            nc.tensor.transpose(
-                                mb[:, il, P * st : P * st + P],
-                                mts[:, st, P * i : P * i + P],
-                                ident[:],
-                            )
-                    pair = slice(2 * ih, 2 * ih + 2)
-                    nc.vector.scalar_tensor_tensor(
-                        out=dpre[:, pair, :],
-                        in0=mb[:],
-                        scalar=-1.0 / A,
-                        in1=sg[:, pair, :],
-                        op0=MULT,
-                        op1=ADD,
-                    )
 
-        for w in range(NW):
-            if w + 3 < NW:
-                load_w(w + 3)
-            if w % 2 == 0 and w // 2 + 1 < A // 2:
-                load_x(w // 2 + 1)
-            prep_w(w)
-            front(w)
-            mid(w)
-            back(w)
+        def leave_psum(w, ih):
+            pp = pps[(w, ih)]
+            pair = slice(2 * ih, 2 * ih + 2)
+            if w == 0:
+                nc.vector.tensor_tensor(
+                    out=sg[:, pair, :],
+                    in0=pp[:],
+                    in1=gam[:].unsqueeze(1).to_broadcast([P, 2, S]),
+                    op=ADD,
+                )
+                return
+            if w == A:
+                nc.vector.scalar_tensor_tensor(
+                    out=dfin[:, pair, :],
+                    in0=pp[:],
+                    scalar=-1.0 / A,
+                    in1=dpre[:, pair, :],
+                    op0=MULT,
+                    op1=ADD,
+                )
+            nc.vector.tensor_tensor(
+                out=outsb[:, pair, w - 1, :],
+                in0=pp[:],
+                in1=b3bc[:, w - 1, :].unsqueeze(1).to_broadcast([P, 2, S]),
+                op=ADD,
+            )
 
-        for i in range(NI):
+        def finish(i):
             for c in range(4):
                 acts = slice(4 * c, 4 * c + 4)
                 nc.vector.tensor_tensor(
@@ -293,3 +268,62 @@ def tile_psicritic_pa_kernel(tc, h1, W2, b2, W3, b3, g1, V2, c2, V3, c3, out):
                     op=ADD,
                 )
                 nc.sync.dma_start(out=outv[:, i, acts, :], in_=outsb[:, i, acts, :])
+
+        for n in range(-2, NW + 1):
+            if live(n - 1):
+                regroup_hidden(n - 1)
+            if n == NW:
+                for st in range(2):
+                    nc.scalar.copy(out=mts[:, st, :], in_=mt[st][:])
+                mbs = []
+                for ih in range(2):
+                    mb = tp_pool.tile([P, 2, S], F32, name="mb", tag="tp")
+                    for il in range(2):
+                        for st in range(2):
+                            nc.tensor.transpose(
+                                mb[:, il, P * st : P * st + P],
+                                mts[:, st, P * (2 * ih + il) : P * (2 * ih + il) + P],
+                                ident[:],
+                            )
+                    mbs.append(mb)
+            if live(n):
+                layer1(n)
+            if live(n - 2):
+                leave_psum(n - 2, 0)
+            if live(n - 1):
+                h2q[n - 1] = quantise(two, F, g2s[n - 1], "h2c", "h2s")
+            if live(n - 2):
+                leave_psum(n - 2, 1)
+            if n == NW:
+                for ih in range(2):
+                    pair = slice(2 * ih, 2 * ih + 2)
+                    nc.vector.scalar_tensor_tensor(
+                        out=dpre[:, pair, :],
+                        in0=mbs[ih][:],
+                        scalar=-1.0 / A,
+                        in1=sg[:, pair, :],
+                        op0=MULT,
+                        op1=ADD,
+                    )
+            if live(n + 2):
+                transpose_x(n + 2)
+            if live(n - 1):
+                layer2(n - 1)
+            if live(n + 2):
+                regroup_weights(n + 2)
+            if live(n + 1):
+                w2q[n + 1] = quantise(two, F, wg[n + 1][0], "w2c", "w2s")
+                h1q[n + 1] = quantise(two, F, g1s[n + 1], "h1c", "h1s")
+                w3q[n + 1] = quantise(three, S, wg[n + 1][1], "w3c", "w3s")
+            if live(n + 2 + RAW_BUFS):
+                load_w2(n + 2 + RAW_BUFS)
+                load_w3(n + 2 + RAW_BUFS)
+            if n >= 0 and n % 2 == 0 and n // 2 + X_BUFS < A // 2:
+                load_x(n // 2 + X_BUFS)
+
+        leave_psum(A, 0)
+        finish(0)
+        finish(1)
+        leave_psum(A, 1)
+        finish(2)
+        finish(3)

@@ -13,13 +13,15 @@ FP8X4 = mybir.dt.float8_e4m3fn_x4
 ADD = mybir.AluOpType.add
 MULT = mybir.AluOpType.mult
 RELU = mybir.ActivationFunctionType.Relu
+IDENT = mybir.ActivationFunctionType.Identity
 
 P = 128
 A = 16
 NI = 4
 F = 512
 S = 256
-HV = 384
+R3V = 192
+B3COL = 4 * (A + 1)
 NW = A + 1
 RAW_BUFS = 4
 X_BUFS = 3
@@ -43,6 +45,7 @@ def tile_psicritic_pa_kernel(tc, h1, W2, b2, W3, b3, g1, V2, c2, V3, c3, out):
         rawp = ctx.enter_context(tc.tile_pool(name="rawp", bufs=RAW_BUFS))
         two = ctx.enter_context(tc.tile_pool(name="two", bufs=2))
         three = ctx.enter_context(tc.tile_pool(name="three", bufs=3))
+        opool = ctx.enter_context(tc.tile_pool(name="opool", bufs=4))
         tp_pool = ctx.enter_context(tc.psum_pool(name="tp_pool", bufs=2))
         l1_pool = ctx.enter_context(tc.psum_pool(name="l1_pool", bufs=2))
         pp_pool = ctx.enter_context(tc.psum_pool(name="pp_pool", bufs=2))
@@ -84,12 +87,18 @@ def tile_psicritic_pa_kernel(tc, h1, W2, b2, W3, b3, g1, V2, c2, V3, c3, out):
             nc.sync.dma_start(out=xt[:], in_=h1v[:, :, 2 * pair : 2 * pair + 2, :])
             xs[pair] = xt
 
+        def load_x_half(pair, al):
+            nc.sync.dma_start(out=xs[pair][:, :, al, :], in_=h1v[:, :, 2 * pair + al, :])
+
         ident = const.tile([P, P], F32, name="ident")
         make_identity(nc, ident[:])
         brow = const.tile([P, P], BF16, name="brow")
         nc.vector.memset(brow[:], 0.0)
         nc.scalar.dma_start(out=brow[0:4, :], in_=c2.rearrange("(t p) -> t p", p=P))
         nc.scalar.dma_start(out=brow[4:68, :], in_=b2.rearrange("a (t p) -> (a t) p", p=P))
+        nc.scalar.dma_start(
+            out=brow[B3COL : B3COL + 2 * A, :], in_=b3.rearrange("a (t p) -> (a t) p", p=P)
+        )
         b3rows = const.tile([P, S], BF16, name="b3rows")
         nc.vector.memset(b3rows[:], 0.0)
         nc.scalar.dma_start(out=b3rows[0:16, :], in_=b3)
@@ -100,19 +109,16 @@ def tile_psicritic_pa_kernel(tc, h1, W2, b2, W3, b3, g1, V2, c2, V3, c3, out):
         nc.vector.memset(lmean[0:16, :], -1.0 / A)
 
         xg = const.tile([P, NI, F], BF16, name="xg")
-        b3bc = const.tile([P, A, S], BF16, name="b3bc")
         load_w2(0)
         nc.sync.dma_start(out=xg[:], in_=g1.rearrange("(i p) k -> p i k", p=P))
         load_w3(0)
+        xs[0] = xpool.tile([P, NI, 2, F], BF16, name="xt")
+        load_x_half(0, 0)
         load_w2(1)
-        load_x(0)
         load_w3(1)
+        load_x_half(0, 1)
         load_w2(2)
         load_w3(2)
-        nc.sync.dma_start(
-            out=b3bc[:].rearrange("p a s -> p (a s)"),
-            in_=b3.rearrange("a s -> (a s)").partition_broadcast(P),
-        )
         load_x(1)
         load_w2(3)
         load_w3(3)
@@ -129,7 +135,7 @@ def tile_psicritic_pa_kernel(tc, h1, W2, b2, W3, b3, g1, V2, c2, V3, c3, out):
         gam = const.tile([P, S], F32, name="gam")
         nc.vector.tensor_copy(out=gam[:], in_=tpg[:, 0, :])
 
-        outsb = const.tile([P, NI, A, S], F32, name="outsb")
+        advt = const.tile([P, A, 2, F], F32, name="advt")
         sg = const.tile([P, NI, S], F32, name="sg")
         dpre = const.tile([P, NI, S], F32, name="dpre")
         dfin = const.tile([P, NI, S], F32, name="dfin")
@@ -148,7 +154,8 @@ def tile_psicritic_pa_kernel(tc, h1, W2, b2, W3, b3, g1, V2, c2, V3, c3, out):
             w2g = two.tile([P, F, 4], BF16, name="w2g", align_bytes=64)
             regroup(nc.vector.tensor_copy, w2g[:], raws[(2, w)][:])
             w3g = two.tile([P, S, 4], BF16, name="w3g", align_bytes=64)
-            regroup(nc.scalar.copy, w3g[:], raws[(3, w)][:])
+            regroup(nc.vector.tensor_copy, w3g[:, 0:R3V, :], raws[(3, w)][:, :, 0:R3V])
+            regroup(nc.scalar.copy, w3g[:, R3V:S, :], raws[(3, w)][:, :, R3V:S])
             wg[w] = (w2g, w3g)
 
         def transpose_x(w):
@@ -172,102 +179,89 @@ def tile_psicritic_pa_kernel(tc, h1, W2, b2, W3, b3, g1, V2, c2, V3, c3, out):
                 )
             g1s[w] = g1t
 
-        def layer1(w):
+        def layer1(w, t):
             w2c, w2s = w2q[w]
             h1c, h1s = h1q[w]
-            planes = two.tile([P, 4, F], BF16, name="planes")
-            for t in range(4):
-                l1 = l1_pool.tile([P, F], F32, name="l1")
-                nc.tensor.matmul_mx(
-                    out=l1[:],
-                    lhsT=w2c[:, P * t : P * t + P].bitcast(FP8X4),
-                    lhsT_scale=w2s[:, P * t : P * t + P],
-                    rhs=h1c[:].bitcast(FP8X4),
-                    rhs_scale=h1s[:],
-                    start=True,
-                    stop=True,
-                )
-                nc.scalar.activation(
-                    out=planes[:, t, :],
-                    in_=l1[:],
-                    func=RELU,
-                    bias=bias2[:, 4 * w + t : 4 * w + t + 1],
-                    scale=1.0,
-                )
-            pls[w] = planes
+            if t == 0:
+                pls[w] = two.tile([P, 4, F], BF16, name="planes")
+            l1 = l1_pool.tile([P, F], F32, name="l1", tag="l1")
+            nc.tensor.matmul_mx(
+                out=l1[:],
+                lhsT=w2c[:, P * t : P * t + P].bitcast(FP8X4),
+                lhsT_scale=w2s[:, P * t : P * t + P],
+                rhs=h1c[:].bitcast(FP8X4),
+                rhs_scale=h1s[:],
+                start=True,
+                stop=True,
+            )
+            nc.scalar.activation(
+                out=pls[w][:, t, :],
+                in_=l1[:],
+                func=RELU,
+                bias=bias2[:, 4 * w + t : 4 * w + t + 1],
+                scale=1.0,
+            )
 
         def regroup_hidden(w):
             g2t = two.tile([P, F, 4], BF16, name="g2t", align_bytes=64)
-            regroup(nc.scalar.copy, g2t[:, HV:F, :], pls[w][:, :, HV:F])
-            regroup(nc.vector.tensor_copy, g2t[:, 0:HV, :], pls[w][:, :, 0:HV])
+            regroup(nc.vector.tensor_copy, g2t[:], pls[w][:])
             g2s[w] = g2t
+
+        def mx(dst, lc, ls, lcols, rc, rs, start, stop):
+            nc.tensor.matmul_mx(
+                out=dst,
+                lhsT=lc[:, lcols].bitcast(FP8X4),
+                lhsT_scale=ls[:, lcols],
+                rhs=rc[:].bitcast(FP8X4),
+                rhs_scale=rs[:],
+                start=start,
+                stop=stop,
+            )
+
+        def batch_major(w, pool, tag):
+            w3c, w3s = w3q[w]
+            h2c, h2s = h2q[w]
+            for ih in range(2):
+                pq = pool.tile([P, 2, S], F32, name="pq", tag=tag)
+                for il in range(2):
+                    i = 2 * ih + il
+                    mx(pq[:, il, :], h2c, h2s, slice(P * i, P * i + P), w3c, w3s, True, True)
+                pps[(w, ih)] = pq
 
         def layer2(w):
             w3c, w3s = w3q[w]
             h2c, h2s = h2q[w]
-            for ih in range(2):
-                pp = pp_pool.tile([P, 2, S], F32, name="pp", tag="pp")
-                for il in range(2):
-                    i = 2 * ih + il
-                    nc.tensor.matmul_mx(
-                        out=pp[:, il, :],
-                        lhsT=h2c[:, P * i : P * i + P].bitcast(FP8X4),
-                        lhsT_scale=h2s[:, P * i : P * i + P],
-                        rhs=w3c[:].bitcast(FP8X4),
-                        rhs_scale=w3s[:],
-                        start=True,
-                        stop=True,
-                    )
-                pps[(w, ih)] = pp
-            if 1 <= w <= A - 1:
-                for st in range(2):
-                    nc.tensor.matmul_mx(
-                        out=mt[st][:],
-                        lhsT=w3c[:, P * st : P * st + P].bitcast(FP8X4),
-                        lhsT_scale=w3s[:, P * st : P * st + P],
-                        rhs=h2c[:].bitcast(FP8X4),
-                        rhs_scale=h2s[:],
-                        start=(w == 1),
-                        stop=(w == A - 1),
-                    )
-
-        def leave_psum(w, ih):
-            pp = pps[(w, ih)]
-            pair = slice(2 * ih, 2 * ih + 2)
             if w == 0:
+                batch_major(w, pp_pool, "pp")
+                return
+            if w == A:
+                batch_major(w, l1_pool, "l1")
+            for st in range(2):
+                cols = slice(P * st, P * st + P)
+                pt = pp_pool.tile([P, F], F32, name="pt", tag="pp")
+                mx(pt[:], w3c, w3s, cols, h2c, h2s, True, True)
+                pps[(-w, st)] = pt
+                if w <= A - 1:
+                    mx(mt[st][:], w3c, w3s, cols, h2c, h2s, w == 1, w == A - 1)
+
+        def leave_psum(w, half):
+            if w == 0:
+                pair = slice(2 * half, 2 * half + 2)
                 nc.vector.tensor_tensor(
                     out=sg[:, pair, :],
-                    in0=pp[:],
+                    in0=pps[(w, half)][:],
                     in1=gam[:].unsqueeze(1).to_broadcast([P, 2, S]),
                     op=ADD,
                 )
                 return
-            if w == A:
-                nc.vector.scalar_tensor_tensor(
-                    out=dfin[:, pair, :],
-                    in0=pp[:],
-                    scalar=-1.0 / A,
-                    in1=dpre[:, pair, :],
-                    op0=MULT,
-                    op1=ADD,
-                )
-            nc.vector.tensor_tensor(
-                out=outsb[:, pair, w - 1, :],
-                in0=pp[:],
-                in1=b3bc[:, w - 1, :].unsqueeze(1).to_broadcast([P, 2, S]),
-                op=ADD,
+            col = B3COL + 2 * (w - 1) + half
+            nc.scalar.activation(
+                out=advt[:, w - 1, half, :],
+                in_=pps[(-w, half)][:],
+                func=IDENT,
+                bias=bias2[:, col : col + 1],
+                scale=1.0,
             )
-
-        def finish(i):
-            for c in range(4):
-                acts = slice(4 * c, 4 * c + 4)
-                nc.vector.tensor_tensor(
-                    out=outsb[:, i, acts, :],
-                    in0=outsb[:, i, acts, :],
-                    in1=dfin[:, i, :].unsqueeze(1).to_broadcast([P, 4, S]),
-                    op=ADD,
-                )
-                nc.sync.dma_start(out=outv[:, i, acts, :], in_=outsb[:, i, acts, :])
 
         for n in range(-2, NW + 1):
             if live(n - 1):
@@ -286,14 +280,16 @@ def tile_psicritic_pa_kernel(tc, h1, W2, b2, W3, b3, g1, V2, c2, V3, c3, out):
                                 ident[:],
                             )
                     mbs.append(mb)
-            if live(n):
-                layer1(n)
-            if live(n - 2):
-                leave_psum(n - 2, 0)
+            for t in range(4):
+                if live(n):
+                    layer1(n, t)
+                if 1 <= t <= 2 and live(n - 2):
+                    leave_psum(n - 2, t - 1)
+            if live(n + 1):
+                w2q[n + 1] = quantise(two, F, wg[n + 1][0], "w2c", "w2s")
+                h1q[n + 1] = quantise(two, F, g1s[n + 1], "h1c", "h1s")
             if live(n - 1):
                 h2q[n - 1] = quantise(two, F, g2s[n - 1], "h2c", "h2s")
-            if live(n - 2):
-                leave_psum(n - 2, 1)
             if n == NW:
                 for ih in range(2):
                     pair = slice(2 * ih, 2 * ih + 2)
@@ -312,8 +308,6 @@ def tile_psicritic_pa_kernel(tc, h1, W2, b2, W3, b3, g1, V2, c2, V3, c3, out):
             if live(n + 2):
                 regroup_weights(n + 2)
             if live(n + 1):
-                w2q[n + 1] = quantise(two, F, wg[n + 1][0], "w2c", "w2s")
-                h1q[n + 1] = quantise(two, F, g1s[n + 1], "h1c", "h1s")
                 w3q[n + 1] = quantise(three, S, wg[n + 1][1], "w3c", "w3s")
             if live(n + 2 + RAW_BUFS):
                 load_w2(n + 2 + RAW_BUFS)
@@ -321,9 +315,35 @@ def tile_psicritic_pa_kernel(tc, h1, W2, b2, W3, b3, g1, V2, c2, V3, c3, out):
             if n >= 0 and n % 2 == 0 and n // 2 + X_BUFS < A // 2:
                 load_x(n // 2 + X_BUFS)
 
-        leave_psum(A, 0)
-        finish(0)
-        finish(1)
-        leave_psum(A, 1)
-        finish(2)
-        finish(3)
+        for half in range(2):
+            pair = slice(2 * half, 2 * half + 2)
+            leave_psum(A, half)
+            nc.vector.scalar_tensor_tensor(
+                out=dfin[:, pair, :],
+                in0=pps[(A, half)][:],
+                scalar=-1.0 / A,
+                in1=dpre[:, pair, :],
+                op0=MULT,
+                op1=ADD,
+            )
+        banks = [(tp_pool, "tp"), (l1_pool, "l1"), (pp_pool, "pp")]
+        for i in range(NI):
+            for c in range(4):
+                ost = opool.tile([P, 4, S], F32, name="ost")
+                for h in range(2):
+                    pool, tag = banks[(8 * i + 2 * c + h) % 3]
+                    fin = pool.tile([P, 2, S], F32, name="fin", tag=tag)
+                    for al in range(2):
+                        for st in range(2):
+                            nc.tensor.transpose(
+                                fin[:, al, P * st : P * st + P],
+                                advt[:, 4 * c + 2 * h + al, st, P * i : P * i + P],
+                                ident[:],
+                            )
+                    nc.vector.tensor_tensor(
+                        out=ost[:, 2 * h : 2 * h + 2, :],
+                        in0=fin[:],
+                        in1=dfin[:, i, :].unsqueeze(1).to_broadcast([P, 2, S]),
+                        op=ADD,
+                    )
+                nc.sync.dma_start(out=outv[:, i, 4 * c : 4 * c + 4, :], in_=ost[:])

@@ -20,7 +20,7 @@ A = 16
 NI = 4
 F = 512
 S = 256
-R3V = 192
+R3V = 256
 B3COL = 4 * (A + 1)
 NW = A + 1
 RAW_BUFS = 4
@@ -155,7 +155,8 @@ def tile_psicritic_pa_kernel(tc, h1, W2, b2, W3, b3, g1, V2, c2, V3, c3, out):
             regroup(nc.vector.tensor_copy, w2g[:], raws[(2, w)][:])
             w3g = two.tile([P, S, 4], BF16, name="w3g", align_bytes=64)
             regroup(nc.vector.tensor_copy, w3g[:, 0:R3V, :], raws[(3, w)][:, :, 0:R3V])
-            regroup(nc.scalar.copy, w3g[:, R3V:S, :], raws[(3, w)][:, :, R3V:S])
+            if R3V < S:
+                regroup(nc.scalar.copy, w3g[:, R3V:S, :], raws[(3, w)][:, :, R3V:S])
             wg[w] = (w2g, w3g)
 
         def transpose_x(w):

@@ -20,8 +20,9 @@ A = 16
 NI = 4
 F = 512
 S = 256
-R3V = 256
+R3V = 192
 B3COL = 4 * (A + 1)
+LAST_SUMMED = 14
 NW = A + 1
 RAW_BUFS = 4
 X_BUFS = 3
@@ -44,8 +45,9 @@ def tile_psicritic_pa_kernel(tc, h1, W2, b2, W3, b3, g1, V2, c2, V3, c3, out):
         xpool = ctx.enter_context(tc.tile_pool(name="xpool", bufs=X_BUFS))
         rawp = ctx.enter_context(tc.tile_pool(name="rawp", bufs=RAW_BUFS))
         two = ctx.enter_context(tc.tile_pool(name="two", bufs=2))
-        three = ctx.enter_context(tc.tile_pool(name="three", bufs=3))
-        opool = ctx.enter_context(tc.tile_pool(name="opool", bufs=4))
+        four = ctx.enter_context(tc.tile_pool(name="four", bufs=4))
+        five = ctx.enter_context(tc.tile_pool(name="five", bufs=5))
+        opool = ctx.enter_context(tc.tile_pool(name="opool", bufs=6))
         tp_pool = ctx.enter_context(tc.psum_pool(name="tp_pool", bufs=2))
         l1_pool = ctx.enter_context(tc.psum_pool(name="l1_pool", bufs=2))
         pp_pool = ctx.enter_context(tc.psum_pool(name="pp_pool", bufs=2))
@@ -63,6 +65,7 @@ def tile_psicritic_pa_kernel(tc, h1, W2, b2, W3, b3, g1, V2, c2, V3, c3, out):
         g2s = {}
         h2q = {}
         pps = {}
+        l1s = {}
 
         def live(w):
             return 0 <= w < NW
@@ -142,6 +145,17 @@ def tile_psicritic_pa_kernel(tc, h1, W2, b2, W3, b3, g1, V2, c2, V3, c3, out):
         mts = const.tile([P, 2, F], F32, name="mts")
         mt = [m_pool.tile([P, F], F32, name="mt%d" % st) for st in range(2)]
 
+        def mx(dst, lc, ls, lcols, rc, rs, start, stop):
+            nc.tensor.matmul_mx(
+                out=dst,
+                lhsT=lc[:, lcols].bitcast(FP8X4),
+                lhsT_scale=ls[:, lcols],
+                rhs=rc[:].bitcast(FP8X4),
+                rhs_scale=rs[:],
+                start=start,
+                stop=stop,
+            )
+
         def quantise(pool, width, src, cname, sname):
             codes = pool.tile([P, width], U32, name=cname, align_bytes=64)
             scales = pool.tile([P, width], U8, name=sname, align_bytes=64)
@@ -155,8 +169,7 @@ def tile_psicritic_pa_kernel(tc, h1, W2, b2, W3, b3, g1, V2, c2, V3, c3, out):
             regroup(nc.vector.tensor_copy, w2g[:], raws[(2, w)][:])
             w3g = two.tile([P, S, 4], BF16, name="w3g", align_bytes=64)
             regroup(nc.vector.tensor_copy, w3g[:, 0:R3V, :], raws[(3, w)][:, :, 0:R3V])
-            if R3V < S:
-                regroup(nc.scalar.copy, w3g[:, R3V:S, :], raws[(3, w)][:, :, R3V:S])
+            regroup(nc.scalar.copy, w3g[:, R3V:S, :], raws[(3, w)][:, :, R3V:S])
             wg[w] = (w2g, w3g)
 
         def transpose_x(w):
@@ -180,44 +193,34 @@ def tile_psicritic_pa_kernel(tc, h1, W2, b2, W3, b3, g1, V2, c2, V3, c3, out):
                 )
             g1s[w] = g1t
 
-        def layer1(w, t):
+        def layer1(w, t, pool, tag):
             w2c, w2s = w2q[w]
             h1c, h1s = h1q[w]
-            if t == 0:
-                pls[w] = two.tile([P, 4, F], BF16, name="planes")
-            l1 = l1_pool.tile([P, F], F32, name="l1", tag="l1")
-            nc.tensor.matmul_mx(
-                out=l1[:],
-                lhsT=w2c[:, P * t : P * t + P].bitcast(FP8X4),
-                lhsT_scale=w2s[:, P * t : P * t + P],
-                rhs=h1c[:].bitcast(FP8X4),
-                rhs_scale=h1s[:],
-                start=True,
-                stop=True,
-            )
+            l1 = pool.tile([P, F], F32, name="l1", tag=tag)
+            mx(l1[:], w2c, w2s, slice(P * t, P * t + P), h1c, h1s, True, True)
+            l1s[(w, t)] = l1
+
+        def relu_out(w, t, cols, dst):
             nc.scalar.activation(
-                out=pls[w][:, t, :],
-                in_=l1[:],
+                out=dst[:, t, :],
+                in_=l1s[(w, t)][:, cols],
                 func=RELU,
                 bias=bias2[:, 4 * w + t : 4 * w + t + 1],
                 scale=1.0,
             )
 
+        def layer1_step(w):
+            pls[w] = two.tile([P, 4, F], BF16, name="planes")
+            for t in range(4):
+                layer1(w, t, l1_pool, "l1")
+                relu_out(w, t, slice(0, F), pls[w])
+                if 1 <= t <= 2 and live(w - 2):
+                    leave_psum(w - 2, t - 1)
+
         def regroup_hidden(w):
             g2t = two.tile([P, F, 4], BF16, name="g2t", align_bytes=64)
             regroup(nc.vector.tensor_copy, g2t[:], pls[w][:])
             g2s[w] = g2t
-
-        def mx(dst, lc, ls, lcols, rc, rs, start, stop):
-            nc.tensor.matmul_mx(
-                out=dst,
-                lhsT=lc[:, lcols].bitcast(FP8X4),
-                lhsT_scale=ls[:, lcols],
-                rhs=rc[:].bitcast(FP8X4),
-                rhs_scale=rs[:],
-                start=start,
-                stop=stop,
-            )
 
         def batch_major(w, pool, tag):
             w3c, w3s = w3q[w]
@@ -229,21 +232,25 @@ def tile_psicritic_pa_kernel(tc, h1, W2, b2, W3, b3, g1, V2, c2, V3, c3, out):
                     mx(pq[:, il, :], h2c, h2s, slice(P * i, P * i + P), w3c, w3s, True, True)
                 pps[(w, ih)] = pq
 
-        def layer2(w):
+        def feature_major(w, st, pool, tag):
             w3c, w3s = w3q[w]
             h2c, h2s = h2q[w]
+            pt = pool.tile([P, F], F32, name="pt", tag=tag)
+            mx(pt[:], w3c, w3s, slice(P * st, P * st + P), h2c, h2s, True, True)
+            pps[(-w, st)] = pt
+
+        def add_to_sum(w, st):
+            w3c, w3s = w3q[w]
+            h2c, h2s = h2q[w]
+            mx(mt[st][:], w3c, w3s, slice(P * st, P * st + P), h2c, h2s, w == 1, w == LAST_SUMMED)
+
+        def layer2(w):
             if w == 0:
                 batch_major(w, pp_pool, "pp")
                 return
-            if w == A:
-                batch_major(w, l1_pool, "l1")
             for st in range(2):
-                cols = slice(P * st, P * st + P)
-                pt = pp_pool.tile([P, F], F32, name="pt", tag="pp")
-                mx(pt[:], w3c, w3s, cols, h2c, h2s, True, True)
-                pps[(-w, st)] = pt
-                if w <= A - 1:
-                    mx(mt[st][:], w3c, w3s, cols, h2c, h2s, w == 1, w == A - 1)
+                feature_major(w, st, pp_pool, "pp")
+                add_to_sum(w, st)
 
         def leave_psum(w, half):
             if w == 0:
@@ -264,44 +271,16 @@ def tile_psicritic_pa_kernel(tc, h1, W2, b2, W3, b3, g1, V2, c2, V3, c3, out):
                 scale=1.0,
             )
 
-        for n in range(-2, NW + 1):
+        for n in range(-2, LAST_SUMMED + 1):
             if live(n - 1):
                 regroup_hidden(n - 1)
-            if n == NW:
-                for st in range(2):
-                    nc.scalar.copy(out=mts[:, st, :], in_=mt[st][:])
-                mbs = []
-                for ih in range(2):
-                    mb = tp_pool.tile([P, 2, S], F32, name="mb", tag="tp")
-                    for il in range(2):
-                        for st in range(2):
-                            nc.tensor.transpose(
-                                mb[:, il, P * st : P * st + P],
-                                mts[:, st, P * (2 * ih + il) : P * (2 * ih + il) + P],
-                                ident[:],
-                            )
-                    mbs.append(mb)
-            for t in range(4):
-                if live(n):
-                    layer1(n, t)
-                if 1 <= t <= 2 and live(n - 2):
-                    leave_psum(n - 2, t - 1)
+            if live(n):
+                layer1_step(n)
             if live(n + 1):
                 w2q[n + 1] = quantise(two, F, wg[n + 1][0], "w2c", "w2s")
                 h1q[n + 1] = quantise(two, F, g1s[n + 1], "h1c", "h1s")
             if live(n - 1):
-                h2q[n - 1] = quantise(two, F, g2s[n - 1], "h2c", "h2s")
-            if n == NW:
-                for ih in range(2):
-                    pair = slice(2 * ih, 2 * ih + 2)
-                    nc.vector.scalar_tensor_tensor(
-                        out=dpre[:, pair, :],
-                        in0=mbs[ih][:],
-                        scalar=-1.0 / A,
-                        in1=sg[:, pair, :],
-                        op0=MULT,
-                        op1=ADD,
-                    )
+                h2q[n - 1] = quantise(four, F, g2s[n - 1], "h2c", "h2s")
             if live(n + 2):
                 transpose_x(n + 2)
             if live(n - 1):
@@ -309,42 +288,129 @@ def tile_psicritic_pa_kernel(tc, h1, W2, b2, W3, b3, g1, V2, c2, V3, c3, out):
             if live(n + 2):
                 regroup_weights(n + 2)
             if live(n + 1):
-                w3q[n + 1] = quantise(three, S, wg[n + 1][1], "w3c", "w3s")
+                w3q[n + 1] = quantise(five, S, wg[n + 1][1], "w3c", "w3s")
             if live(n + 2 + RAW_BUFS):
                 load_w2(n + 2 + RAW_BUFS)
                 load_w3(n + 2 + RAW_BUFS)
             if n >= 0 and n % 2 == 0 and n // 2 + X_BUFS < A // 2:
                 load_x(n // 2 + X_BUFS)
 
-        for half in range(2):
-            pair = slice(2 * half, 2 * half + 2)
-            leave_psum(A, half)
-            nc.vector.scalar_tensor_tensor(
-                out=dfin[:, pair, :],
-                in0=pps[(A, half)][:],
-                scalar=-1.0 / A,
-                in1=dpre[:, pair, :],
-                op0=MULT,
-                op1=ADD,
+        w_a, w_b, w_c = LAST_SUMMED, LAST_SUMMED + 1, LAST_SUMMED + 2
+        regroup_hidden(w_a)
+        layer1_step(w_b)
+        w2q[w_c] = quantise(two, F, wg[w_c][0], "w2c", "w2s")
+        h1q[w_c] = quantise(two, F, g1s[w_c], "h1c", "h1s")
+        layer1(w_c, 0, tp_pool, "tp")
+        layer1(w_c, 1, tp_pool, "tp")
+        h2q[w_a] = quantise(four, F, g2s[w_a], "h2c", "h2s")
+        add_to_sum(w_a, 0)
+        add_to_sum(w_a, 1)
+        layer1(w_c, 2, l1_pool, "l1")
+        layer1(w_c, 3, l1_pool, "l1")
+        w3q[w_c] = quantise(five, S, wg[w_c][1], "w3c", "w3s")
+
+        halves = [slice(0, S), slice(S, F)]
+        plh = [None, None]
+        g2h = [None, None]
+        plh[0] = two.tile([P, 4, S], BF16, name="planes")
+        for t in range(4):
+            relu_out(w_c, t, halves[0], plh[0])
+        for st in range(2):
+            nc.scalar.copy(out=mts[:, st, :], in_=mt[st][:])
+        regroup_hidden(w_b)
+        plh[1] = two.tile([P, 4, S], BF16, name="planes")
+        for t in range(4):
+            relu_out(w_c, t, halves[1], plh[1])
+
+        h2c_c = four.tile([P, F], U32, name="h2c", align_bytes=64)
+        h2s_c = four.tile([P, F], U8, name="h2s", align_bytes=64)
+        h2q[w_c] = (h2c_c, h2s_c)
+
+        def regroup_last(h):
+            g2h[h] = two.tile([P, S, 4], BF16, name="g2t", align_bytes=64)
+            regroup(nc.vector.tensor_copy, g2h[h][:], plh[h][:])
+
+        def quantise_last(h):
+            nc.vector.quantize_mx(
+                out=h2c_c[:, halves[h]].bitcast(FP8X4),
+                scales=h2s_c[:, halves[h]],
+                in_=g2h[h][:].rearrange("p n t -> p (n t)"),
             )
-        banks = [(tp_pool, "tp"), (l1_pool, "l1"), (pp_pool, "pp")]
-        for i in range(NI):
-            for c in range(4):
-                ost = opool.tile([P, 4, S], F32, name="ost")
-                for h in range(2):
-                    pool, tag = banks[(8 * i + 2 * c + h) % 3]
-                    fin = pool.tile([P, 2, S], F32, name="fin", tag=tag)
-                    for al in range(2):
-                        for st in range(2):
-                            nc.tensor.transpose(
-                                fin[:, al, P * st : P * st + P],
-                                advt[:, 4 * c + 2 * h + al, st, P * i : P * i + P],
-                                ident[:],
-                            )
-                    nc.vector.tensor_tensor(
-                        out=ost[:, 2 * h : 2 * h + 2, :],
-                        in0=fin[:],
-                        in1=dfin[:, i, :].unsqueeze(1).to_broadcast([P, 2, S]),
-                        op=ADD,
+
+        mbs = [None, None]
+        pqs = [None, None]
+
+        def turn_sum(ih):
+            mbs[ih] = m_pool.tile([P, 2, S], F32, name="mb", tag="mt%d" % ih)
+            for il in range(2):
+                for st in range(2):
+                    nc.tensor.transpose(
+                        mbs[ih][:, il, P * st : P * st + P],
+                        mts[:, st, P * (2 * ih + il) : P * (2 * ih + il) + P],
+                        ident[:],
                     )
-                nc.sync.dma_start(out=outv[:, i, 4 * c : 4 * c + 4, :], in_=ost[:])
+
+        def last_two_products(ih):
+            pqs[ih] = pp_pool.tile([P, 2, S], F32, name="pq", tag="pp")
+            for il in range(2):
+                cols = slice(P * (2 * ih + il), P * (2 * ih + il) + P)
+                for w in (w_b, w_c):
+                    mx(pqs[ih][:, il, :], h2q[w][0], h2q[w][1], cols, w3q[w][0], w3q[w][1], w == w_b, w == w_c)
+
+        def minus_mean(dst, src, base, ih):
+            pair = slice(2 * ih, 2 * ih + 2)
+            nc.vector.scalar_tensor_tensor(
+                out=dst[:, pair, :], in0=src[:], scalar=-1.0 / A, in1=base[:, pair, :], op0=MULT, op1=ADD
+            )
+
+        def late_product(w):
+            for st in range(2):
+                feature_major(w, st, m_pool, "mt%d" % st)
+                leave_psum(w, st)
+
+        regroup_last(0)
+        h2q[w_b] = quantise(four, F, g2s[w_b], "h2c", "h2s")
+        quantise_last(0)
+        turn_sum(0)
+        last_two_products(0)
+        minus_mean(dpre, mbs[0], sg, 0)
+        minus_mean(dfin, pqs[0], dpre, 0)
+
+        chunks = (
+            [(i, c) for i in (0, 1) for c in range(3)]
+            + [(i, c) for i in (2, 3) for c in range(3)]
+            + [(i, 3) for i in range(NI)]
+        )
+        banks = [(l1_pool, "l1"), (tp_pool, "tp")]
+        for k, (i, c) in enumerate(chunks):
+            ost = opool.tile([P, 4, S], F32, name="ost")
+            for h in range(2):
+                pool, tag = banks[h]
+                fin = pool.tile([P, 2, S], F32, name="fin", tag=tag)
+                for al in range(2):
+                    for st in range(2):
+                        nc.tensor.transpose(
+                            fin[:, al, P * st : P * st + P],
+                            advt[:, 4 * c + 2 * h + al, st, P * i : P * i + P],
+                            ident[:],
+                        )
+                nc.vector.tensor_tensor(
+                    out=ost[:, 2 * h : 2 * h + 2, :],
+                    in0=fin[:],
+                    in1=dfin[:, i, :].unsqueeze(1).to_broadcast([P, 2, S]),
+                    op=ADD,
+                )
+            nc.sync.dma_start(out=outv[:, i, 4 * c : 4 * c + 4, :], in_=ost[:])
+            if k == 0:
+                regroup_last(1)
+            if k == 1:
+                turn_sum(1)
+                quantise_last(1)
+            if k == 2:
+                minus_mean(dpre, mbs[1], sg, 1)
+            if k == 3:
+                last_two_products(1)
+            if k == 4:
+                minus_mean(dfin, pqs[1], dpre, 1)
+            if k in (5, 7, 9):
+                late_product(w_a + (k - 5) // 2)

@@ -20,7 +20,9 @@ A = 16
 NI = 4
 F = 512
 S = 256
-R3V = 192
+R3V_FIRST = 128
+R3V = 224
+FIRST = 5
 B3COL = 4 * (A + 1)
 LAST_SUMMED = 14
 NW = A + 1
@@ -168,8 +170,9 @@ def tile_psicritic_pa_kernel(tc, h1, W2, b2, W3, b3, g1, V2, c2, V3, c3, out):
             w2g = two.tile([P, F, 4], BF16, name="w2g", align_bytes=64)
             regroup(nc.vector.tensor_copy, w2g[:], raws[(2, w)][:])
             w3g = two.tile([P, S, 4], BF16, name="w3g", align_bytes=64)
-            regroup(nc.vector.tensor_copy, w3g[:, 0:R3V, :], raws[(3, w)][:, :, 0:R3V])
-            regroup(nc.scalar.copy, w3g[:, R3V:S, :], raws[(3, w)][:, :, R3V:S])
+            cut = R3V_FIRST if w < FIRST else R3V
+            regroup(nc.vector.tensor_copy, w3g[:, 0:cut, :], raws[(3, w)][:, :, 0:cut])
+            regroup(nc.scalar.copy, w3g[:, cut:S, :], raws[(3, w)][:, :, cut:S])
             wg[w] = (w2g, w3g)
 
         def transpose_x(w):

@@ -20,9 +20,7 @@ A = 16
 NI = 4
 F = 512
 S = 256
-R3V_FIRST = 128
-R3V = 224
-FIRST = 5
+R3V = 192
 B3COL = 4 * (A + 1)
 LAST_SUMMED = 14
 NW = A + 1
@@ -170,9 +168,8 @@ def tile_psicritic_pa_kernel(tc, h1, W2, b2, W3, b3, g1, V2, c2, V3, c3, out):
             w2g = two.tile([P, F, 4], BF16, name="w2g", align_bytes=64)
             regroup(nc.vector.tensor_copy, w2g[:], raws[(2, w)][:])
             w3g = two.tile([P, S, 4], BF16, name="w3g", align_bytes=64)
-            cut = R3V_FIRST if w < FIRST else R3V
-            regroup(nc.vector.tensor_copy, w3g[:, 0:cut, :], raws[(3, w)][:, :, 0:cut])
-            regroup(nc.scalar.copy, w3g[:, cut:S, :], raws[(3, w)][:, :, cut:S])
+            regroup(nc.vector.tensor_copy, w3g[:, 0:R3V, :], raws[(3, w)][:, :, 0:R3V])
+            regroup(nc.scalar.copy, w3g[:, R3V:S, :], raws[(3, w)][:, :, R3V:S])
             wg[w] = (w2g, w3g)
 
         def transpose_x(w):
@@ -215,10 +212,12 @@ def tile_psicritic_pa_kernel(tc, h1, W2, b2, W3, b3, g1, V2, c2, V3, c3, out):
         def layer1_step(w):
             pls[w] = two.tile([P, 4, F], BF16, name="planes")
             for t in range(4):
-                layer1(w, t, l1_pool, "l1")
+                if t >= 2 or w == 0:
+                    layer1(w, t, l1_pool, "l1")
                 relu_out(w, t, slice(0, F), pls[w])
-                if 1 <= t <= 2 and live(w - 2):
-                    leave_psum(w - 2, t - 1)
+                if t == 1 and live(w - 2):
+                    leave_psum(w - 2, 0)
+                    leave_psum(w - 2, 1)
 
         def regroup_hidden(w):
             g2t = two.tile([P, F, 4], BF16, name="g2t", align_bytes=64)
@@ -247,13 +246,14 @@ def tile_psicritic_pa_kernel(tc, h1, W2, b2, W3, b3, g1, V2, c2, V3, c3, out):
             h2c, h2s = h2q[w]
             mx(mt[st][:], w3c, w3s, slice(P * st, P * st + P), h2c, h2s, w == 1, w == LAST_SUMMED)
 
-        def layer2(w):
+        def layer2_and_next_layer1(w):
             if w == 0:
                 batch_major(w, pp_pool, "pp")
-                return
             for st in range(2):
-                feature_major(w, st, pp_pool, "pp")
-                add_to_sum(w, st)
+                layer1(w + 2, st, l1_pool, "l1")
+                if w >= 1:
+                    feature_major(w, st, pp_pool, "pp")
+                    add_to_sum(w, st)
 
         def leave_psum(w, half):
             if w == 0:
@@ -286,8 +286,8 @@ def tile_psicritic_pa_kernel(tc, h1, W2, b2, W3, b3, g1, V2, c2, V3, c3, out):
                 h2q[n - 1] = quantise(four, F, g2s[n - 1], "h2c", "h2s")
             if live(n + 2):
                 transpose_x(n + 2)
-            if live(n - 1):
-                layer2(n - 1)
+            if n >= 0:
+                layer2_and_next_layer1(n - 1)
             if live(n + 2):
                 regroup_weights(n + 2)
             if live(n + 1):
@@ -299,18 +299,18 @@ def tile_psicritic_pa_kernel(tc, h1, W2, b2, W3, b3, g1, V2, c2, V3, c3, out):
                 load_x(n // 2 + X_BUFS)
 
         w_a, w_b, w_c = LAST_SUMMED, LAST_SUMMED + 1, LAST_SUMMED + 2
-        regroup_hidden(w_a)
-        layer1_step(w_b)
         w2q[w_c] = quantise(two, F, wg[w_c][0], "w2c", "w2s")
         h1q[w_c] = quantise(two, F, g1s[w_c], "h1c", "h1s")
+        regroup_hidden(w_a)
+        layer1_step(w_b)
         layer1(w_c, 0, tp_pool, "tp")
         layer1(w_c, 1, tp_pool, "tp")
+        w3q[w_c] = quantise(five, S, wg[w_c][1], "w3c", "w3s")
         h2q[w_a] = quantise(four, F, g2s[w_a], "h2c", "h2s")
-        add_to_sum(w_a, 0)
-        add_to_sum(w_a, 1)
         layer1(w_c, 2, l1_pool, "l1")
         layer1(w_c, 3, l1_pool, "l1")
-        w3q[w_c] = quantise(five, S, wg[w_c][1], "w3c", "w3s")
+        add_to_sum(w_a, 0)
+        add_to_sum(w_a, 1)
 
         halves = [slice(0, S), slice(S, F)]
         plh = [None, None]

@@ -52,7 +52,6 @@ def tile_psicritic_pa_kernel(tc, h1, W2, b2, W3, b3, g1, V2, c2, V3, c3, out):
         l1_pool = ctx.enter_context(tc.psum_pool(name="l1_pool", bufs=2))
         pp_pool = ctx.enter_context(tc.psum_pool(name="pp_pool", bufs=2))
         m_pool = ctx.enter_context(tc.psum_pool(name="m_pool", bufs=1))
-        ctx.enter_context(tc.manual_schedule())
 
         raws = {}
         xs = {}
@@ -212,12 +211,10 @@ def tile_psicritic_pa_kernel(tc, h1, W2, b2, W3, b3, g1, V2, c2, V3, c3, out):
         def layer1_step(w):
             pls[w] = two.tile([P, 4, F], BF16, name="planes")
             for t in range(4):
-                if t >= 2 or w == 0:
-                    layer1(w, t, l1_pool, "l1")
+                layer1(w, t, l1_pool, "l1")
                 relu_out(w, t, slice(0, F), pls[w])
-                if t == 1 and live(w - 2):
-                    leave_psum(w - 2, 0)
-                    leave_psum(w - 2, 1)
+                if 1 <= t <= 2 and live(w - 2):
+                    leave_psum(w - 2, t - 1)
 
         def regroup_hidden(w):
             g2t = two.tile([P, F, 4], BF16, name="g2t", align_bytes=64)
@@ -246,14 +243,13 @@ def tile_psicritic_pa_kernel(tc, h1, W2, b2, W3, b3, g1, V2, c2, V3, c3, out):
             h2c, h2s = h2q[w]
             mx(mt[st][:], w3c, w3s, slice(P * st, P * st + P), h2c, h2s, w == 1, w == LAST_SUMMED)
 
-        def layer2_and_next_layer1(w):
+        def layer2(w):
             if w == 0:
                 batch_major(w, pp_pool, "pp")
+                return
             for st in range(2):
-                layer1(w + 2, st, l1_pool, "l1")
-                if w >= 1:
-                    feature_major(w, st, pp_pool, "pp")
-                    add_to_sum(w, st)
+                feature_major(w, st, pp_pool, "pp")
+                add_to_sum(w, st)
 
         def leave_psum(w, half):
             if w == 0:
@@ -286,8 +282,8 @@ def tile_psicritic_pa_kernel(tc, h1, W2, b2, W3, b3, g1, V2, c2, V3, c3, out):
                 h2q[n - 1] = quantise(four, F, g2s[n - 1], "h2c", "h2s")
             if live(n + 2):
                 transpose_x(n + 2)
-            if n >= 0:
-                layer2_and_next_layer1(n - 1)
+            if live(n - 1):
+                layer2(n - 1)
             if live(n + 2):
                 regroup_weights(n + 2)
             if live(n + 1):
@@ -299,18 +295,18 @@ def tile_psicritic_pa_kernel(tc, h1, W2, b2, W3, b3, g1, V2, c2, V3, c3, out):
                 load_x(n // 2 + X_BUFS)
 
         w_a, w_b, w_c = LAST_SUMMED, LAST_SUMMED + 1, LAST_SUMMED + 2
-        w2q[w_c] = quantise(two, F, wg[w_c][0], "w2c", "w2s")
-        h1q[w_c] = quantise(two, F, g1s[w_c], "h1c", "h1s")
         regroup_hidden(w_a)
         layer1_step(w_b)
+        w2q[w_c] = quantise(two, F, wg[w_c][0], "w2c", "w2s")
+        h1q[w_c] = quantise(two, F, g1s[w_c], "h1c", "h1s")
         layer1(w_c, 0, tp_pool, "tp")
         layer1(w_c, 1, tp_pool, "tp")
-        w3q[w_c] = quantise(five, S, wg[w_c][1], "w3c", "w3s")
         h2q[w_a] = quantise(four, F, g2s[w_a], "h2c", "h2s")
-        layer1(w_c, 2, l1_pool, "l1")
-        layer1(w_c, 3, l1_pool, "l1")
         add_to_sum(w_a, 0)
         add_to_sum(w_a, 1)
+        layer1(w_c, 2, l1_pool, "l1")
+        layer1(w_c, 3, l1_pool, "l1")
+        w3q[w_c] = quantise(five, S, wg[w_c][1], "w3c", "w3s")
 
         halves = [slice(0, S), slice(S, F)]
         plh = [None, None]

from contextlib import ExitStack

import concourse.mybir as mybir
from concourse.masks import make_identity

FLOPS = 17 * (2 * 512 * 512 * 512 + 2 * 512 * 512 * 256)

F32 = mybir.dt.float32
BF16 = mybir.dt.bfloat16
U32 = mybir.dt.uint32
U8 = mybir.dt.uint8
FP8X4 = mybir.dt.float8_e4m3fn_x4
ADD = mybir.AluOpType.add
MULT = mybir.AluOpType.mult
RELU = mybir.ActivationFunctionType.Relu
IDENT = mybir.ActivationFunctionType.Identity

P = 128
A = 16
NI = 4
F = 512
S = 256
R3V = 192
B3COL = 4 * (A + 1)
LAST_SUMMED = 14
NW = A + 1
RAW_BUFS = 4
X_BUFS = 3


def regroup(engine_copy, dst, src):
    engine_copy(
        out=dst.rearrange("p (c i) t -> p c t i", i=4),
        in_=src.rearrange("p t (c i) -> p c t i", i=4),
    )


def tile_psicritic_pa_kernel(tc, h1, W2, b2, W3, b3, g1, V2, c2, V3, c3, out):
    nc = tc.nc
    h1v = h1.rearrange("(i p) a k -> p i a k", p=P)
    outv = out.rearrange("(i p) a s -> p i a s", p=P)

    with ExitStack() as ctx:
        const = ctx.enter_context(tc.tile_pool(name="const", bufs=1))
        xpool = ctx.enter_context(tc.tile_pool(name="xpool", bufs=X_BUFS))
        rawp = ctx.enter_context(tc.tile_pool(name="rawp", bufs=RAW_BUFS))
        two = ctx.enter_context(tc.tile_pool(name="two", bufs=2))
        four = ctx.enter_context(tc.tile_pool(name="four", bufs=4))
        five = ctx.enter_context(tc.tile_pool(name="five", bufs=5))
        opool = ctx.enter_context(tc.tile_pool(name="opool", bufs=6))
        tp_pool = ctx.enter_context(tc.psum_pool(name="tp_pool", bufs=2))
        l1_pool = ctx.enter_context(tc.psum_pool(name="l1_pool", bufs=2))
        pp_pool = ctx.enter_context(tc.psum_pool(name="pp_pool", bufs=2))
        m_pool = ctx.enter_context(tc.psum_pool(name="m_pool", bufs=1))

        raws = {}
        xs = {}
        wg = {}
        w2q = {}
        w3q = {}
        g1s = {}
        h1q = {}
        pls = {}
        g2s = {}
        h2q = {}
        pps = {}
        l1s = {}

        def live(w):
            return 0 <= w < NW

        def load_w2(w):
            w2raw = rawp.tile([P, 4, F], BF16, name="w2raw")
            nc.sync.dma_start(
                out=w2raw[:].rearrange("p (u e) n -> p u (e n)", u=2),
                in_=(V2 if w == 0 else W2[w - 1]).rearrange("(u p e) n -> p u (e n)", u=2, e=2),
            )
            raws[(2, w)] = w2raw

        def load_w3(w):
            w3raw = rawp.tile([P, 4, S], BF16, name="w3raw")
            nc.sync.dma_start(
                out=w3raw[:], in_=(V3 if w == 0 else W3[w - 1]).rearrange("(t p) s -> p t s", p=P)
            )
            raws[(3, w)] = w3raw

        def load_x(pair):
            xt = xpool.tile([P, NI, 2, F], BF16, name="xt")
            nc.sync.dma_start(out=xt[:], in_=h1v[:, :, 2 * pair : 2 * pair + 2, :])
            xs[pair] = xt

        def load_x_half(pair, al):
            nc.sync.dma_start(out=xs[pair][:, :, al, :], in_=h1v[:, :, 2 * pair + al, :])

        ident = const.tile([P, P], F32, name="ident")
        make_identity(nc, ident[:])
        brow = const.tile([P, P], BF16, name="brow")
        nc.vector.memset(brow[:], 0.0)
        nc.scalar.dma_start(out=brow[0:4, :], in_=c2.rearrange("(t p) -> t p", p=P))
        nc.scalar.dma_start(out=brow[4:68, :], in_=b2.rearrange("a (t p) -> (a t) p", p=P))
        nc.scalar.dma_start(
            out=brow[B3COL : B3COL + 2 * A, :], in_=b3.rearrange("a (t p) -> (a t) p", p=P)
        )
        b3rows = const.tile([P, S], BF16, name="b3rows")
        nc.vector.memset(b3rows[:], 0.0)
        nc.scalar.dma_start(out=b3rows[0:16, :], in_=b3)
        nc.scalar.dma_start(out=b3rows[16:17, :], in_=c3.rearrange("(o s) -> o s", o=1))
        lmean = const.tile([P, P], BF16, name="lmean")
        nc.vector.memset(lmean[:], 0.0)
        nc.vector.memset(lmean[0:17, :], 1.0)
        nc.vector.memset(lmean[0:16, :], -1.0 / A)

        xg = const.tile([P, NI, F], BF16, name="xg")
        load_w2(0)
        nc.sync.dma_start(out=xg[:], in_=g1.rearrange("(i p) k -> p i k", p=P))
        load_w3(0)
        xs[0] = xpool.tile([P, NI, 2, F], BF16, name="xt")
        load_x_half(0, 0)
        load_w2(1)
        load_w3(1)
        load_x_half(0, 1)
        load_w2(2)
        load_w3(2)
        load_x(1)
        load_w2(3)
        load_w3(3)
        load_x(2)

        browf = const.tile([P, P], F32, name="browf")
        nc.vector.tensor_copy(out=browf[:], in_=brow[:])
        tpb = pp_pool.tile([P, 2, S], F32, name="tpb", tag="pp")
        nc.tensor.transpose(tpb[:, 0, 0:P], browf[:], ident[:])
        bias2 = const.tile([P, P], F32, name="bias2")
        nc.vector.tensor_copy(out=bias2[:], in_=tpb[:, 0, 0:P])
        tpg = pp_pool.tile([P, 2, S], F32, name="tpg", tag="pp")
        nc.tensor.matmul(tpg[:, 0, :], lhsT=lmean[:], rhs=b3rows[:], start=True, stop=True)
        gam = const.tile([P, S], F32, name="gam")
        nc.vector.tensor_copy(out=gam[:], in_=tpg[:, 0, :])

        advt = const.tile([P, A, 2, F], F32, name="advt")
        sg = const.tile([P, NI, S], F32, name="sg")
        dpre = const.tile([P, NI, S], F32, name="dpre")
        dfin = const.tile([P, NI, S], F32, name="dfin")
        mts = const.tile([P, 2, F], F32, name="mts")
        mt = [m_pool.tile([P, F], F32, name="mt%d" % st) for st in range(2)]

        def mx(dst, lc, ls, lcols, rc, rs, start, stop):
            nc.tensor.matmul_mx(
                out=dst,
                lhsT=lc[:, lcols].bitcast(FP8X4),
                lhsT_scale=ls[:, lcols],
                rhs=rc[:].bitcast(FP8X4),
                rhs_scale=rs[:],
                start=start,
                stop=stop,
            )

        def quantise(pool, width, src, cname, sname):
            codes = pool.tile([P, width], U32, name=cname, align_bytes=64)
            scales = pool.tile([P, width], U8, name=sname, align_bytes=64)
            nc.vector.quantize_mx(
                out=codes[:].bitcast(FP8X4), scales=scales[:], in_=src[:].rearrange("p n t -> p (n t)")
            )
            return codes, scales

        def regroup_weights(w):
            w2g = two.tile([P, F, 4], BF16, name="w2g", align_bytes=64)
            regroup(nc.vector.tensor_copy, w2g[:], raws[(2, w)][:])
            w3g = two.tile([P, S, 4], BF16, name="w3g", align_bytes=64)
            regroup(nc.vector.tensor_copy, w3g[:, 0:R3V, :], raws[(3, w)][:, :, 0:R3V])
            regroup(nc.scalar.copy, w3g[:, R3V:S, :], raws[(3, w)][:, :, R3V:S])
            wg[w] = (w2g, w3g)

        def transpose_x(w):
            if w == 0:
                xw = xg[:].bitcast(F32)
            else:
                xw = xs[(w - 1) // 2][:].bitcast(F32)[:, :, (w - 1) % 2, :]
            g1t = two.tile([P, F, 4], BF16, name="g1t", align_bytes=64)
            g1w = g1t[:].bitcast(F32)
            for ih in range(2):
                tp = tp_pool.tile([P, 2, S], F32, name="tp", tag="tp")
                for il in range(2):
                    for u in range(2):
                        nc.tensor.transpose(
                            tp[:, u, P * il : P * il + P],
                            xw[:, 2 * ih + il, P * u : P * u + P],
                            ident[:],
                        )
                nc.scalar.copy(
                    out=g1w[:, S * ih : S * ih + S, :], in_=tp[:].rearrange("p u b -> p b u")
                )
            g1s[w] = g1t

        def layer1(w, t, pool, tag):
            w2c, w2s = w2q[w]
            h1c, h1s = h1q[w]
            l1 = pool.tile([P, F], F32, name="l1", tag=tag)
            mx(l1[:], w2c, w2s, slice(P * t, P * t + P), h1c, h1s, True, True)
            l1s[(w, t)] = l1

        def relu_out(w, t, cols, dst):
            nc.scalar.activation(
                out=dst[:, t, :],
                in_=l1s[(w, t)][:, cols],
                func=RELU,
                bias=bias2[:, 4 * w + t : 4 * w + t + 1],
                scale=1.0,
            )

        def layer1_step(w):
            pls[w] = two.tile([P, 4, F], BF16, name="planes")
            for t in range(4):
                layer1(w, t, l1_pool, "l1")
                relu_out(w, t, slice(0, F), pls[w])
                if 1 <= t <= 2 and live(w - 2):
                    leave_psum(w - 2, t - 1)

        def regroup_hidden(w):
            g2t = two.tile([P, F, 4], BF16, name="g2t", align_bytes=64)
            regroup(nc.vector.tensor_copy, g2t[:], pls[w][:])
            g2s[w] = g2t

        def batch_major(w, pool, tag):
            w3c, w3s = w3q[w]
            h2c, h2s = h2q[w]
            for ih in range(2):
                pq = pool.tile([P, 2, S], F32, name="pq", tag=tag)
                for il in range(2):
                    i = 2 * ih + il
                    mx(pq[:, il, :], h2c, h2s, slice(P * i, P * i + P), w3c, w3s, True, True)
                pps[(w, ih)] = pq

        def feature_major(w, st, pool, tag):
            w3c, w3s = w3q[w]
            h2c, h2s = h2q[w]
            pt = pool.tile([P, F], F32, name="pt", tag=tag)
            mx(pt[:], w3c, w3s, slice(P * st, P * st + P), h2c, h2s, True, True)
            pps[(-w, st)] = pt

        def add_to_sum(w, st):
            w3c, w3s = w3q[w]
            h2c, h2s = h2q[w]
            mx(mt[st][:], w3c, w3s, slice(P * st, P * st + P), h2c, h2s, w == 1, w == LAST_SUMMED)

        def layer2(w):
            if w == 0:
                batch_major(w, pp_pool, "pp")
                return
            for st in range(2):
                feature_major(w, st, pp_pool, "pp")
                add_to_sum(w, st)

        def leave_psum(w, half):
            if w == 0:
                pair = slice(2 * half, 2 * half + 2)
                nc.vector.tensor_tensor(
                    out=sg[:, pair, :],
                    in0=pps[(w, half)][:],
                    in1=gam[:].unsqueeze(1).to_broadcast([P, 2, S]),
                    op=ADD,
                )
                return
            col = B3COL + 2 * (w - 1) + half
            nc.scalar.activation(
                out=advt[:, w - 1, half, :],
                in_=pps[(-w, half)][:],
                func=IDENT,
                bias=bias2[:, col : col + 1],
                scale=1.0,
            )

        for n in range(-2, LAST_SUMMED + 1):
            if live(n - 1):
                regroup_hidden(n - 1)
            if live(n):
                layer1_step(n)
            if live(n + 1):
                w2q[n + 1] = quantise(two, F, wg[n + 1][0], "w2c", "w2s")
                h1q[n + 1] = quantise(two, F, g1s[n + 1], "h1c", "h1s")
            if live(n - 1):
                h2q[n - 1] = quantise(four, F, g2s[n - 1], "h2c", "h2s")
            if live(n + 2):
                transpose_x(n + 2)
            if live(n - 1):
                layer2(n - 1)
            if live(n + 2):
                regroup_weights(n + 2)
            if live(n + 1):
                w3q[n + 1] = quantise(five, S, wg[n + 1][1], "w3c", "w3s")
            if live(n + 2 + RAW_BUFS):
                load_w2(n + 2 + RAW_BUFS)
                load_w3(n + 2 + RAW_BUFS)
            if n >= 0 and n % 2 == 0 and n // 2 + X_BUFS < A // 2:
                load_x(n // 2 + X_BUFS)

        w_a, w_b, w_c = LAST_SUMMED, LAST_SUMMED + 1, LAST_SUMMED + 2
        regroup_hidden(w_a)
        layer1_step(w_b)
        w2q[w_c] = quantise(two, F, wg[w_c][0], "w2c", "w2s")
        h1q[w_c] = quantise(two, F, g1s[w_c], "h1c", "h1s")
        layer1(w_c, 0, tp_pool, "tp")
        layer1(w_c, 1, tp_pool, "tp")
        h2q[w_a] = quantise(four, F, g2s[w_a], "h2c", "h2s")
        add_to_sum(w_a, 0)
        add_to_sum(w_a, 1)
        layer1(w_c, 2, l1_pool, "l1")
        layer1(w_c, 3, l1_pool, "l1")
        w3q[w_c] = quantise(five, S, wg[w_c][1], "w3c", "w3s")

        halves = [slice(0, S), slice(S, F)]
        plh = [None, None]
        g2h = [None, None]
        plh[0] = two.tile([P, 4, S], BF16, name="planes")
        for t in range(4):
            relu_out(w_c, t, halves[0], plh[0])
        for st in range(2):
            nc.scalar.copy(out=mts[:, st, :], in_=mt[st][:])
        regroup_hidden(w_b)
        plh[1] = two.tile([P, 4, S], BF16, name="planes")
        for t in range(4):
            relu_out(w_c, t, halves[1], plh[1])

        h2c_c = four.tile([P, F], U32, name="h2c", align_bytes=64)
        h2s_c = four.tile([P, F], U8, name="h2s", align_bytes=64)
        h2q[w_c] = (h2c_c, h2s_c)

        def regroup_last(h):
            g2h[h] = two.tile([P, S, 4], BF16, name="g2t", align_bytes=64)
            regroup(nc.vector.tensor_copy, g2h[h][:], plh[h][:])

        def quantise_last(h):
            nc.vector.quantize_mx(
                out=h2c_c[:, halves[h]].bitcast(FP8X4),
                scales=h2s_c[:, halves[h]],
                in_=g2h[h][:].rearrange("p n t -> p (n t)"),
            )

        mbs = [None, None]
        pqs = [None, None]

        def turn_sum(ih):
            mbs[ih] = m_pool.tile([P, 2, S], F32, name="mb", tag="mt%d" % ih)
            for il in range(2):
                for st in range(2):
                    nc.tensor.transpose(
                        mbs[ih][:, il, P * st : P * st + P],
                        mts[:, st, P * (2 * ih + il) : P * (2 * ih + il) + P],
                        ident[:],
                    )

        def last_two_products(ih):
            pqs[ih] = pp_pool.tile([P, 2, S], F32, name="pq", tag="pp")
            for il in range(2):
                cols = slice(P * (2 * ih + il), P * (2 * ih + il) + P)
                for w in (w_b, w_c):
                    mx(pqs[ih][:, il, :], h2q[w][0], h2q[w][1], cols, w3q[w][0], w3q[w][1], w == w_b, w == w_c)

        def minus_mean(dst, src, base, ih):
            pair = slice(2 * ih, 2 * ih + 2)
            nc.vector.scalar_tensor_tensor(
                out=dst[:, pair, :], in0=src[:], scalar=-1.0 / A, in1=base[:, pair, :], op0=MULT, op1=ADD
            )

        def late_product(w):
            for st in range(2):
                feature_major(w, st, m_pool, "mt%d" % st)
                leave_psum(w, st)

        regroup_last(0)
        h2q[w_b] = quantise(four, F, g2s[w_b], "h2c", "h2s")
        quantise_last(0)
        turn_sum(0)
        last_two_products(0)
        minus_mean(dpre, mbs[0], sg, 0)
        minus_mean(dfin, pqs[0], dpre, 0)

        chunks = (
            [(i, c) for i in (0, 1) for c in range(3)]
            + [(i, c) for i in (2, 3) for c in range(3)]
            + [(i, 3) for i in range(NI)]
        )
        banks = [(l1_pool, "l1"), (tp_pool, "tp")]
        for k, (i, c) in enumerate(chunks):
            ost = opool.tile([P, 4, S], F32, name="ost")
            for h in range(2):
                pool, tag = banks[h]
                fin = pool.tile([P, 2, S], F32, name="fin", tag=tag)
                for al in range(2):
                    for st in range(2):
                        nc.tensor.transpose(
                            fin[:, al, P * st : P * st + P],
                            advt[:, 4 * c + 2 * h + al, st, P * i : P * i + P],
                            ident[:],
                        )
                nc.vector.tensor_tensor(
                    out=ost[:, 2 * h : 2 * h + 2, :],
                    in0=fin[:],
                    in1=dfin[:, i, :].unsqueeze(1).to_broadcast([P, 2, S]),
                    op=ADD,
                )
            nc.sync.dma_start(out=outv[:, i, 4 * c : 4 * c + 4, :], in_=ost[:])
            if k == 0:
                regroup_last(1)
            if k == 1:
                turn_sum(1)
                quantise_last(1)
            if k == 2:
                minus_mean(dpre, mbs[1], sg, 1)
            if k == 3:
                last_two_products(1)
            if k == 4:
                minus_mean(dfin, pqs[1], dpre, 1)
            if k in (5, 7, 9):
                late_product(w_a + (k - 5) // 2)
